import numpy as np
import ml_dtypes


def mxq(x, axis, fmt="e4m3"):
    dtype, down = {"e4m3": (ml_dtypes.float8_e4m3fn, 7), "e5m2": (ml_dtypes.float8_e5m2, 14)}[fmt]
    v = np.moveaxis(np.asarray(x, np.float32).astype(ml_dtypes.bfloat16).astype(np.float64), axis, -1)
    blocks = v.reshape(v.shape[:-1] + (-1, 32))
    amax = np.abs(blocks).max(-1, keepdims=True)
    byte = np.maximum(np.where(amax > 0, np.frexp(amax)[1] - 1 + 127, 0) - down, 1)
    scale = np.exp2(byte - 127.0)
    codes = (blocks / scale).astype(np.float32).astype(dtype).astype(np.float64)
    return np.moveaxis((codes * scale).reshape(v.shape), -1, axis)


WIDE = False


def mx_kscale(k):
    if not WIDE:
        return np.ones(k)
    levels = np.array([10, -10, 5, -5, 0])
    a = np.random.permutation(np.resize(levels, k // 512 * 4)).reshape(k // 512, 4)
    idx = np.arange(k)
    return np.exp2(a[idx // 512, idx % 128 // 32])


BF16 = ml_dtypes.bfloat16


def bf(x):
    return np.asarray(x, np.float32).astype(BF16)


def f64(x):
    return np.asarray(x).astype(np.float64)


B, D, U = 2048, 512, 128


def sigmoid(v):
    return 1.0 / (1.0 + np.exp(-v))


def setup_inputs():
    s = mx_kscale(D)
    inp = {"pre_layer": bf(np.random.standard_normal((2, B, U))), "x": bf(np.random.standard_normal((B, D)) * s)}
    for n in ("W_i", "W_f", "W_o", "W_c"):
        inp[n] = bf(np.random.standard_normal((D, U)) / np.sqrt(D) / s[:, None])
    for n in ("U_i", "U_f", "U_o", "U_c"):
        inp[n] = bf(np.random.standard_normal((U, U)) / np.sqrt(U))
    return inp


def reference(pre_layer, x, W_i, W_f, W_o, W_c, U_i, U_f, U_o, U_c):
    pre = f64(pre_layer)
    pre_h, pre_c = pre[0], pre[1]
    W = np.concatenate([f64(W_i), f64(W_f), f64(W_o), f64(W_c)], axis=1)
    Uw = np.concatenate([f64(U_i), f64(U_f), f64(U_o), f64(U_c)], axis=1)
    gates = (mxq(f64(x), 1, "e4m3") @ mxq(W, 0, "e4m3")) + pre_h @ Uw
    zi, zf, zo, zc = np.split(gates, 4, axis=1)
    i_t = sigmoid(zi)
    f_t = sigmoid(zf)
    o_t = sigmoid(zo)
    n_c_t = np.tanh(zc)
    c = f_t * pre_c + i_t * n_c_t
    h = o_t * np.tanh(c)
    return np.stack([h, c])

@@ -1,0 +1,181 @@
+from contextlib import ExitStack
+
+import concourse.mybir as mybir
+from concourse.masks import make_identity
+
+FLOPS = 2 * 2048 * 512 * 512 + 2 * 2048 * 128 * 512
+
+F32 = mybir.dt.float32
+BF16 = mybir.dt.bfloat16
+U32 = mybir.dt.uint32
+U8 = mybir.dt.uint8
+FP8X4 = mybir.dt.float8_e4m3fn_x4
+ACT = mybir.ActivationFunctionType
+ALU = mybir.AluOpType
+
+P = 128
+NT = 16
+D = 512
+U = 128
+G4 = 4 * U
+
+X_CHUNKS = [2, 2, 4, 4, 4]
+GROUPS = [4, 4, 4, 4]
+XT_COPY = ["v", "v", "v", "v", "v", "v", "v", "v"]
+MT_COPY = ["v", "s", "v", "s"]
+
+
+def tile_lstm_kernel(tc, pre_layer, x, W_i, W_f, W_o, W_c, U_i, U_f, U_o, U_c, out):
+    nc = tc.nc
+    with ExitStack() as ctx:
+        keep = ctx.enter_context(tc.tile_pool(name="keep", bufs=1))
+        work = ctx.enter_context(tc.tile_pool(name="work", bufs=3))
+        psum = ctx.enter_context(tc.psum_pool(name="psum", bufs=2))
+
+        xv = x.rearrange("(p t) k -> p t k", t=NT)
+        prev = pre_layer.rearrange("s (p t) u -> s p t u", t=NT)
+        outv = out.rearrange("s (p t) u -> s p t u", t=NT)
+
+        x_tiles = []
+        x_of_tile = {}
+        t0 = 0
+        for ci, n in enumerate(X_CHUNKS):
+            xc = keep.tile([P, n * D], BF16, name="xc%d" % ci)
+            x_tiles.append((xc, t0, n))
+            for j in range(n):
+                x_of_tile[t0 + j] = (xc, j)
+            t0 += n
+
+        w_raw = keep.tile([P, 4, 4 * U], BF16, name="w_raw")
+        u_sb = keep.tile([P, G4], BF16, name="u_sb")
+        ph_sb = keep.tile([P, NT, U], BF16, name="ph_sb")
+        pc_sb = keep.tile([P, NT, U], BF16, name="pc_sb")
+
+        def load_x(ci):
+            xc, s, n = x_tiles[ci]
+            nc.sync.dma_start(out=xc[:].rearrange("p (t k) -> p t k", t=n), in_=xv[:, s : s + n, :])
+
+        load_x(0)
+        for g, w in enumerate((W_i, W_f, W_o, W_c)):
+            nc.sync.dma_start(
+                out=w_raw[:, g, :].rearrange("q (u m) -> q u m", u=2),
+                in_=w.rearrange("(u q e) c -> q u (e c)", u=2, q=P, e=2),
+            )
+        nc.scalar.dma_start(out=ph_sb[:], in_=prev[0])
+        for g, uw in enumerate((U_i, U_f, U_o, U_c)):
+            nc.scalar.dma_start(out=u_sb[:, g * U : (g + 1) * U], in_=uw)
+        for ci in range(1, len(X_CHUNKS)):
+            load_x(ci)
+        nc.scalar.dma_start(out=pc_sb[:], in_=prev[1])
+
+        ident_f = keep.tile([P, P], F32, name="ident_f")
+        make_identity(nc, ident_f[:])
+        ident_b = keep.tile([P, P], BF16, name="ident_b")
+        make_identity(nc, ident_b[:])
+        warm = keep.tile([P, 1], F32, name="warm")
+        nc.vector.memset(warm[:], 0.0)
+        warm2 = keep.tile([P, 1], F32, name="warm2")
+        nc.scalar.activation(out=warm2[:], in_=warm[:], func=ACT.Sigmoid)
+
+        wg = keep.tile([P, 4 * G4], BF16, name="wg", align_bytes=64)
+        wq = keep.tile([P, G4], U32, name="wq", align_bytes=64)
+        ws = keep.tile([P, G4], U8, name="ws", align_bytes=64)
+        nc.vector.tensor_copy(
+            out=wg[:].rearrange("p (g c t) -> p g c t", g=4, c=U, t=4),
+            in_=w_raw[:].rearrange("p g (t c) -> p g c t", t=4),
+        )
+
+        xq = keep.tile([P, NT * P], U32, name="xq", align_bytes=64)
+        xs = keep.tile([P, NT * P], U8, name="xs", align_bytes=64)
+        hT_sb = keep.tile([P, NT * P], BF16, name="hT_sb")
+
+        def x_pair(i):
+            xt = psum.tile([P, 2, 2, P], F32, name="xt", tag="tr")
+            for j in range(2):
+                xc, jj = x_of_tile[2 * i + j]
+                xw = xc[:].bitcast(F32)
+                for u in range(2):
+                    c0 = jj * (D // 2) + u * P
+                    nc.tensor.transpose(xt[:, j, u, :], xw[:, c0 : c0 + P], ident_f[:])
+            xg = work.tile([P, 2 * D], BF16, name="xg", align_bytes=64)
+            dst = xg[:].bitcast(F32).rearrange("p (j r u) -> p j r u", j=2, r=P, u=2)
+            src = xt[:].rearrange("p j u r -> p j r u")
+            if XT_COPY[i] == "v":
+                nc.vector.tensor_copy(out=dst, in_=src)
+            else:
+                nc.scalar.copy(out=dst, in_=src)
+            return xg
+
+        def x_quant(i, xg):
+            cols = slice(2 * i * P, (2 * i + 2) * P)
+            nc.vector.quantize_mx(out=xq[:, cols].bitcast(FP8X4), scales=xs[:, cols], in_=xg[:])
+
+        def h_half(i):
+            ht = psum.tile([P, 8, P], BF16, name="ht", tag="tr")
+            for j in range(8):
+                nc.tensor.transpose(ht[:, j, :], ph_sb[:, 8 * i + j, :], ident_b[:])
+            nc.scalar.copy(
+                out=hT_sb[:, 8 * i * P : (8 * i + 8) * P], in_=ht[:].rearrange("p j r -> p (j r)")
+            )
+
+        xg0 = x_pair(0)
+        nc.vector.quantize_mx(out=wq[:].bitcast(FP8X4), scales=ws[:], in_=wg[:])
+        x_quant(0, xg0)
+        h_half(0)
+        h_half(1)
+
+        pairs_done = 1
+        t0 = 0
+        for n in GROUPS:
+            while pairs_done * 2 < t0 + n:
+                xg = x_pair(pairs_done)
+                x_quant(pairs_done, xg)
+                pairs_done += 1
+            mts = []
+            for g in range(4):
+                mt = psum.tile([P, n * P], F32, name="mt", tag="mt", bufs=3)
+                nc.tensor.matmul_mx(
+                    out=mt[:],
+                    lhsT=wq[:, g * U : (g + 1) * U].bitcast(FP8X4),
+                    lhsT_scale=ws[:, g * U : (g + 1) * U],
+                    rhs=xq[:, t0 * P : (t0 + n) * P].bitcast(FP8X4),
+                    rhs_scale=xs[:, t0 * P : (t0 + n) * P],
+                    start=True,
+                    stop=True,
+                )
+                mt_sb = work.tile([P, n * P], F32, name="mt_sb%d" % g, tag="mt_sb%d" % g, bufs=2)
+                if MT_COPY[g] == "v":
+                    nc.vector.tensor_copy(out=mt_sb[:], in_=mt[:])
+                else:
+                    nc.scalar.copy(out=mt_sb[:], in_=mt[:])
+                mts.append(mt_sb)
+            a = work.tile([P, n, G4], F32, name="a", tag="a")
+            for j in range(n):
+                t = t0 + j
+                cols = slice(t * P, (t + 1) * P)
+                zt = psum.tile([P, G4], F32, name="zt", tag="zt", bufs=3)
+                nc.tensor.matmul(out=zt[:], lhsT=hT_sb[:, cols], rhs=u_sb[:], start=True, stop=False)
+                for g in range(4):
+                    nc.tensor.matmul(
+                        out=zt[:, g * U : (g + 1) * U],
+                        lhsT=mts[g][:, j * P : (j + 1) * P],
+                        rhs=ident_f[:],
+                        is_transpose=True,
+                        start=False,
+                        stop=(g == 3),
+                    )
+                nc.scalar.activation(out=a[:, j, 0 : 3 * U], in_=zt[:, 0 : 3 * U], func=ACT.Sigmoid)
+                nc.scalar.activation(out=a[:, j, 3 * U : G4], in_=zt[:, 3 * U : G4], func=ACT.Tanh)
+            fa = work.tile([P, n, U], F32, name="fa", tag="fa")
+            nc.vector.tensor_tensor(out=fa[:], in0=a[:, :, U : 2 * U], in1=pc_sb[:, t0 : t0 + n, :], op=ALU.mult)
+            ib = work.tile([P, n, U], F32, name="ib", tag="ib")
+            nc.vector.tensor_tensor(out=ib[:], in0=a[:, :, 0:U], in1=a[:, :, 3 * U : G4], op=ALU.mult)
+            c_sb = work.tile([P, n, U], F32, name="c_sb", tag="c_sb")
+            nc.vector.tensor_tensor(out=c_sb[:], in0=fa[:], in1=ib[:], op=ALU.add)
+            nc.sync.dma_start(out=outv[1, :, t0 : t0 + n, :], in_=c_sb[:])
+            tc_sb = work.tile([P, n, U], F32, name="tc_sb", tag="tc_sb")
+            nc.scalar.activation(out=tc_sb[:], in_=c_sb[:], func=ACT.Tanh)
+            h_sb = work.tile([P, n, U], F32, name="h_sb", tag="h_sb")
+            nc.vector.tensor_tensor(out=h_sb[:], in0=a[:, :, 2 * U : 3 * U], in1=tc_sb[:], op=ALU.mult)
+            nc.sync.dma_start(out=outv[0, :, t0 : t0 + n, :], in_=h_sb[:])
+            t0 += n

@@ -15,58 +15,55 @@ ALU = mybir.AluOpType
 
 P = 128
 NT = 16
+NP = NT // 2
 D = 512
 U = 128
 G4 = 4 * U
 
-X_CHUNKS = [2, 2, 4, 4, 4]
-GROUPS = [4, 4, 4, 4]
-XT_COPY = ["v", "v", "v", "v", "v", "v", "v", "v"]
-MT_COPY = ["v", "s", "v", "s"]
+MX_AHEAD = 2
+FRONT_FIRST = 3
+FRONT_STEP = 2
+H1_AT = 2
 
 
 def tile_lstm_kernel(tc, pre_layer, x, W_i, W_f, W_o, W_c, U_i, U_f, U_o, U_c, out):
     nc = tc.nc
     with ExitStack() as ctx:
         keep = ctx.enter_context(tc.tile_pool(name="keep", bufs=1))
-        work = ctx.enter_context(tc.tile_pool(name="work", bufs=3))
+        work = ctx.enter_context(tc.tile_pool(name="work", bufs=4))
         psum = ctx.enter_context(tc.psum_pool(name="psum", bufs=2))
+        ctx.enter_context(tc.manual_schedule())
 
         xv = x.rearrange("(p t) k -> p t k", t=NT)
         prev = pre_layer.rearrange("s (p t) u -> s p t u", t=NT)
         outv = out.rearrange("s (p t) u -> s p t u", t=NT)
 
-        x_tiles = []
-        x_of_tile = {}
-        t0 = 0
-        for ci, n in enumerate(X_CHUNKS):
-            xc = keep.tile([P, n * D], BF16, name="xc%d" % ci)
-            x_tiles.append((xc, t0, n))
-            for j in range(n):
-                x_of_tile[t0 + j] = (xc, j)
-            t0 += n
-
-        w_raw = keep.tile([P, 4, 4 * U], BF16, name="w_raw")
+        x_sb = [keep.tile([P, 2 * D], BF16, name="x%d" % k) for k in range(NP)]
+        w_raw = [keep.tile([P, 4 * U], BF16, name="w_raw%d" % g) for g in range(4)]
         u_sb = keep.tile([P, G4], BF16, name="u_sb")
-        ph_sb = keep.tile([P, NT, U], BF16, name="ph_sb")
+        ph_sb = [keep.tile([P, 8, U], BF16, name="ph%d" % i) for i in range(2)]
         pc_sb = keep.tile([P, NT, U], BF16, name="pc_sb")
 
-        def load_x(ci):
-            xc, s, n = x_tiles[ci]
-            nc.sync.dma_start(out=xc[:].rearrange("p (t k) -> p t k", t=n), in_=xv[:, s : s + n, :])
+        def load_x(k):
+            nc.sync.dma_start(
+                out=x_sb[k][:].rearrange("p (t k) -> p t k", t=2), in_=xv[:, 2 * k : 2 * k + 2, :]
+            )
 
         load_x(0)
+        nc.scalar.dma_start(out=ph_sb[0][:], in_=prev[0, :, 0:8, :])
         for g, w in enumerate((W_i, W_f, W_o, W_c)):
             nc.sync.dma_start(
-                out=w_raw[:, g, :].rearrange("q (u m) -> q u m", u=2),
+                out=w_raw[g][:].rearrange("q (u m) -> q u m", u=2),
                 in_=w.rearrange("(u q e) c -> q u (e c)", u=2, q=P, e=2),
             )
-        nc.scalar.dma_start(out=ph_sb[:], in_=prev[0])
         for g, uw in enumerate((U_i, U_f, U_o, U_c)):
             nc.scalar.dma_start(out=u_sb[:, g * U : (g + 1) * U], in_=uw)
-        for ci in range(1, len(X_CHUNKS)):
-            load_x(ci)
-        nc.scalar.dma_start(out=pc_sb[:], in_=prev[1])
+        for k in (1, 2, 3, 4, 5):
+            load_x(k)
+        nc.sync.dma_start(out=pc_sb[:], in_=prev[1])
+        load_x(6)
+        load_x(7)
+        nc.sync.dma_start(out=ph_sb[1][:], in_=prev[0, :, 8:16, :])
 
         ident_f = keep.tile([P, P], F32, name="ident_f")
         make_identity(nc, ident_f[:])
@@ -80,102 +77,159 @@ def tile_lstm_kernel(tc, pre_layer, x, W_i, W_f, W_o, W_c, U_i, U_f, U_o, U_c, o
         wg = keep.tile([P, 4 * G4], BF16, name="wg", align_bytes=64)
         wq = keep.tile([P, G4], U32, name="wq", align_bytes=64)
         ws = keep.tile([P, G4], U8, name="ws", align_bytes=64)
-        nc.vector.tensor_copy(
-            out=wg[:].rearrange("p (g c t) -> p g c t", g=4, c=U, t=4),
-            in_=w_raw[:].rearrange("p g (t c) -> p g c t", t=4),
-        )
-
         xq = keep.tile([P, NT * P], U32, name="xq", align_bytes=64)
         xs = keep.tile([P, NT * P], U8, name="xs", align_bytes=64)
-        hT_sb = keep.tile([P, NT * P], BF16, name="hT_sb")
+        hT_sb = [keep.tile([P, 8 * P], BF16, name="hT%d" % i) for i in range(2)]
 
-        def x_pair(i):
-            xt = psum.tile([P, 2, 2, P], F32, name="xt", tag="tr")
+        def w_regroup(g):
+            nc.vector.tensor_copy(
+                out=wg[:, g * 4 * U : (g + 1) * 4 * U].rearrange("p (c t) -> p c t", t=4),
+                in_=w_raw[g][:].rearrange("p (t c) -> p c t", t=4),
+            )
+
+        def w_quant(g):
+            nc.vector.quantize_mx(
+                out=wq[:, g * U : (g + 1) * U].bitcast(FP8X4),
+                scales=ws[:, g * U : (g + 1) * U],
+                in_=wg[:, g * 4 * U : (g + 1) * 4 * U],
+            )
+
+        xg_of = {}
+
+        def x_front(k):
+            xt = psum.tile([P, 2, 2, P], F32, name="xt", tag="tr", bufs=2)
+            xw = x_sb[k][:].bitcast(F32)
             for j in range(2):
-                xc, jj = x_of_tile[2 * i + j]
-                xw = xc[:].bitcast(F32)
                 for u in range(2):
-                    c0 = jj * (D // 2) + u * P
+                    c0 = j * (D // 2) + u * P
                     nc.tensor.transpose(xt[:, j, u, :], xw[:, c0 : c0 + P], ident_f[:])
-            xg = work.tile([P, 2 * D], BF16, name="xg", align_bytes=64)
+            xg = work.tile([P, 2 * D], BF16, name="xg", tag="xg", align_bytes=64)
             dst = xg[:].bitcast(F32).rearrange("p (j r u) -> p j r u", j=2, r=P, u=2)
             src = xt[:].rearrange("p j u r -> p j r u")
-            if XT_COPY[i] == "v":
+            if k % 2 == 1:
                 nc.vector.tensor_copy(out=dst, in_=src)
             else:
                 nc.scalar.copy(out=dst, in_=src)
-            return xg
+            xg_of[k] = xg
 
-        def x_quant(i, xg):
-            cols = slice(2 * i * P, (2 * i + 2) * P)
-            nc.vector.quantize_mx(out=xq[:, cols].bitcast(FP8X4), scales=xs[:, cols], in_=xg[:])
+        def x_quant(k):
+            cols = slice(2 * k * P, (2 * k + 2) * P)
+            nc.vector.quantize_mx(out=xq[:, cols].bitcast(FP8X4), scales=xs[:, cols], in_=xg_of[k][:])
 
         def h_half(i):
-            ht = psum.tile([P, 8, P], BF16, name="ht", tag="tr")
+            ht = psum.tile([P, 8, P], BF16, name="ht", tag="tr", bufs=2)
             for j in range(8):
-                nc.tensor.transpose(ht[:, j, :], ph_sb[:, 8 * i + j, :], ident_b[:])
-            nc.scalar.copy(
-                out=hT_sb[:, 8 * i * P : (8 * i + 8) * P], in_=ht[:].rearrange("p j r -> p (j r)")
-            )
+                nc.tensor.transpose(ht[:, j, :], ph_sb[i][:, j, :], ident_b[:])
+            nc.scalar.copy(out=hT_sb[i][:], in_=ht[:].rearrange("p j r -> p (j r)"))
 
-        xg0 = x_pair(0)
-        nc.vector.quantize_mx(out=wq[:].bitcast(FP8X4), scales=ws[:], in_=wg[:])
-        x_quant(0, xg0)
-        h_half(0)
-        h_half(1)
+        mt_of = {}
 
-        pairs_done = 1
-        t0 = 0
-        for n in GROUPS:
-            while pairs_done * 2 < t0 + n:
-                xg = x_pair(pairs_done)
-                x_quant(pairs_done, xg)
-                pairs_done += 1
-            mts = []
-            for g in range(4):
-                mt = psum.tile([P, n * P], F32, name="mt", tag="mt", bufs=3)
-                nc.tensor.matmul_mx(
-                    out=mt[:],
-                    lhsT=wq[:, g * U : (g + 1) * U].bitcast(FP8X4),
-                    lhsT_scale=ws[:, g * U : (g + 1) * U],
-                    rhs=xq[:, t0 * P : (t0 + n) * P].bitcast(FP8X4),
-                    rhs_scale=xs[:, t0 * P : (t0 + n) * P],
-                    start=True,
-                    stop=True,
-                )
-                mt_sb = work.tile([P, n * P], F32, name="mt_sb%d" % g, tag="mt_sb%d" % g, bufs=2)
-                if MT_COPY[g] == "v":
+        def mx_pair(k):
+            cols = slice(2 * k * P, (2 * k + 2) * P)
+            for b in range(2):
+                mt = psum.tile([P, 2, 2 * P], F32, name="mt", tag="mt", bufs=4)
+                for gg in range(2):
+                    g = 2 * b + gg
+                    nc.tensor.matmul_mx(
+                        out=mt[:, gg, :],
+                        lhsT=wq[:, g * U : (g + 1) * U].bitcast(FP8X4),
+                        lhsT_scale=ws[:, g * U : (g + 1) * U],
+                        rhs=xq[:, cols].bitcast(FP8X4),
+                        rhs_scale=xs[:, cols],
+                        start=True,
+                        stop=True,
+                    )
+                mt_sb = work.tile([P, 2, 2 * P], F32, name="mt_sb%d" % b, tag="mt_sb%d" % b)
+                if b == 0:
                     nc.vector.tensor_copy(out=mt_sb[:], in_=mt[:])
                 else:
                     nc.scalar.copy(out=mt_sb[:], in_=mt[:])
-                mts.append(mt_sb)
-            a = work.tile([P, n, G4], F32, name="a", tag="a")
-            for j in range(n):
-                t = t0 + j
-                cols = slice(t * P, (t + 1) * P)
-                zt = psum.tile([P, G4], F32, name="zt", tag="zt", bufs=3)
-                nc.tensor.matmul(out=zt[:], lhsT=hT_sb[:, cols], rhs=u_sb[:], start=True, stop=False)
-                for g in range(4):
-                    nc.tensor.matmul(
-                        out=zt[:, g * U : (g + 1) * U],
-                        lhsT=mts[g][:, j * P : (j + 1) * P],
-                        rhs=ident_f[:],
-                        is_transpose=True,
-                        start=False,
-                        stop=(g == 3),
-                    )
-                nc.scalar.activation(out=a[:, j, 0 : 3 * U], in_=zt[:, 0 : 3 * U], func=ACT.Sigmoid)
-                nc.scalar.activation(out=a[:, j, 3 * U : G4], in_=zt[:, 3 * U : G4], func=ACT.Tanh)
-            fa = work.tile([P, n, U], F32, name="fa", tag="fa")
-            nc.vector.tensor_tensor(out=fa[:], in0=a[:, :, U : 2 * U], in1=pc_sb[:, t0 : t0 + n, :], op=ALU.mult)
-            ib = work.tile([P, n, U], F32, name="ib", tag="ib")
+                mt_of[(k, b)] = mt_sb
+
+        a_of = {}
+
+        def gates(t):
+            k, j = t // 2, t % 2
+            if j == 0:
+                a_new = work.tile([P, 2, G4], F32, name="a", tag="a")
+                a_of[k] = a_new
+            a = a_of[k]
+            zt = psum.tile([P, G4], F32, name="zt", tag="zt", bufs=2)
+            nc.tensor.matmul(
+                out=zt[:], lhsT=hT_sb[t // 8][:, (t % 8) * P : (t % 8 + 1) * P], rhs=u_sb[:], start=True, stop=False
+            )
+            for g in range(4):
+                nc.tensor.matmul(
+                    out=zt[:, g * U : (g + 1) * U],
+                    lhsT=mt_of[(k, g // 2)][:, g % 2, j * P : (j + 1) * P],
+                    rhs=ident_f[:],
+                    is_transpose=True,
+                    start=False,
+                    stop=(g == 3),
+                )
+            nc.scalar.activation(out=a[:, j, 0 : 3 * U], in_=zt[:, 0 : 3 * U], func=ACT.Sigmoid)
+            nc.scalar.activation(out=a[:, j, 3 * U : G4], in_=zt[:, 3 * U : G4], func=ACT.Tanh)
+
+        tc_of = {}
+
+        def cell(k):
+            a = a_of[k]
+            fa = work.tile([P, 2, U], F32, name="fa", tag="fa")
+            nc.vector.tensor_tensor(out=fa[:], in0=a[:, :, U : 2 * U], in1=pc_sb[:, 2 * k : 2 * k + 2, :], op=ALU.mult)
+            ib = work.tile([P, 2, U], F32, name="ib", tag="ib")
             nc.vector.tensor_tensor(out=ib[:], in0=a[:, :, 0:U], in1=a[:, :, 3 * U : G4], op=ALU.mult)
-            c_sb = work.tile([P, n, U], F32, name="c_sb", tag="c_sb")
+            c_sb = work.tile([P, 2, U], F32, name="c_sb", tag="c_sb")
             nc.vector.tensor_tensor(out=c_sb[:], in0=fa[:], in1=ib[:], op=ALU.add)
-            nc.sync.dma_start(out=outv[1, :, t0 : t0 + n, :], in_=c_sb[:])
-            tc_sb = work.tile([P, n, U], F32, name="tc_sb", tag="tc_sb")
+            nc.sync.dma_start(out=outv[1, :, 2 * k : 2 * k + 2, :], in_=c_sb[:])
+            tc_sb = work.tile([P, 2, U], F32, name="tc_sb", tag="tc_sb")
             nc.scalar.activation(out=tc_sb[:], in_=c_sb[:], func=ACT.Tanh)
-            h_sb = work.tile([P, n, U], F32, name="h_sb", tag="h_sb")
-            nc.vector.tensor_tensor(out=h_sb[:], in0=a[:, :, 2 * U : 3 * U], in1=tc_sb[:], op=ALU.mult)
-            nc.sync.dma_start(out=outv[0, :, t0 : t0 + n, :], in_=h_sb[:])
-            t0 += n
+            tc_of[k] = tc_sb
+
+        def hidden(k):
+            h_sb = work.tile([P, 2, U], F32, name="h_sb", tag="h_sb")
+            nc.vector.tensor_tensor(out=h_sb[:], in0=a_of[k][:, :, 2 * U : 3 * U], in1=tc_of[k][:], op=ALU.mult)
+            nc.sync.dma_start(out=outv[0, :, 2 * k : 2 * k + 2, :], in_=h_sb[:])
+
+        for g in range(4):
+            w_regroup(g)
+            if g > 0:
+                w_quant(g - 1)
+        w_quant(3)
+
+        state = {"front": 0, "quant": 0}
+
+        def front(n):
+            for i in range(n):
+                if state["front"] < NP:
+                    x_front(state["front"])
+                    state["front"] += 1
+                    if state["front"] - 1 > state["quant"]:
+                        x_quant(state["quant"])
+                        state["quant"] += 1
+
+        def flush_quant():
+            while state["quant"] < state["front"]:
+                x_quant(state["quant"])
+                state["quant"] += 1
+
+        front(FRONT_FIRST)
+        h_half(0)
+        flush_quant()
+        for k in range(MX_AHEAD):
+            mx_pair(k)
+        for s in range(NP + 2):
+            if s < NP:
+                gates(2 * s)
+                gates(2 * s + 1)
+            if 0 <= s - 1 < NP:
+                cell(s - 1)
+            if 0 <= s - 2 < NP:
+                hidden(s - 2)
+            if state["front"] < NP:
+                front(FRONT_STEP)
+                if state["front"] >= NP:
+                    flush_quant()
+            if s == H1_AT:
+                h_half(1)
+            if s + MX_AHEAD < NP:
+                mx_pair(s + MX_AHEAD)

@@ -24,13 +24,14 @@ MX_AHEAD = 2
 FRONT_FIRST = 3
 FRONT_STEP = 2
 H1_AT = 2
+G_PAIRS = 6
 
 
 def tile_lstm_kernel(tc, pre_layer, x, W_i, W_f, W_o, W_c, U_i, U_f, U_o, U_c, out):
     nc = tc.nc
     with ExitStack() as ctx:
         keep = ctx.enter_context(tc.tile_pool(name="keep", bufs=1))
-        work = ctx.enter_context(tc.tile_pool(name="work", bufs=4))
+        work = ctx.enter_context(tc.tile_pool(name="work", bufs=5))
         psum = ctx.enter_context(tc.psum_pool(name="psum", bufs=2))
         ctx.enter_context(tc.manual_schedule())
 
@@ -127,7 +128,7 @@ def tile_lstm_kernel(tc, pre_layer, x, W_i, W_f, W_o, W_c, U_i, U_f, U_o, U_c, o
         def mx_pair(k):
             cols = slice(2 * k * P, (2 * k + 2) * P)
             for b in range(2):
-                mt = psum.tile([P, 2, 2 * P], F32, name="mt", tag="mt", bufs=4)
+                mt = psum.tile([P, 2, 2 * P], F32, name="mt", tag="mt", bufs=3)
                 for gg in range(2):
                     g = 2 * b + gg
                     nc.tensor.matmul_mx(
@@ -140,7 +141,7 @@ def tile_lstm_kernel(tc, pre_layer, x, W_i, W_f, W_o, W_c, U_i, U_f, U_o, U_c, o
                         stop=True,
                     )
                 mt_sb = work.tile([P, 2, 2 * P], F32, name="mt_sb%d" % b, tag="mt_sb%d" % b)
-                if b == 0:
+                if b == 0 or k % 2 == 1:
                     nc.vector.tensor_copy(out=mt_sb[:], in_=mt[:])
                 else:
                     nc.scalar.copy(out=mt_sb[:], in_=mt[:])
@@ -154,7 +155,7 @@ def tile_lstm_kernel(tc, pre_layer, x, W_i, W_f, W_o, W_c, U_i, U_f, U_o, U_c, o
                 a_new = work.tile([P, 2, G4], F32, name="a", tag="a")
                 a_of[k] = a_new
             a = a_of[k]
-            zt = psum.tile([P, G4], F32, name="zt", tag="zt", bufs=2)
+            zt = psum.tile([P, G4], F32, name="zt", tag="zt", bufs=3)
             nc.tensor.matmul(
                 out=zt[:], lhsT=hT_sb[t // 8][:, (t % 8) * P : (t % 8 + 1) * P], rhs=u_sb[:], start=True, stop=False
             )
@@ -171,18 +172,23 @@ def tile_lstm_kernel(tc, pre_layer, x, W_i, W_f, W_o, W_c, U_i, U_f, U_o, U_c, o
             nc.scalar.activation(out=a[:, j, 3 * U : G4], in_=zt[:, 3 * U : G4], func=ACT.Tanh)
 
         tc_of = {}
+        c_of = {}
 
         def cell(k):
+            eng = nc.gpsimd if k < G_PAIRS else nc.vector
             a = a_of[k]
             fa = work.tile([P, 2, U], F32, name="fa", tag="fa")
-            nc.vector.tensor_tensor(out=fa[:], in0=a[:, :, U : 2 * U], in1=pc_sb[:, 2 * k : 2 * k + 2, :], op=ALU.mult)
+            eng.tensor_tensor(out=fa[:], in0=a[:, :, U : 2 * U], in1=pc_sb[:, 2 * k : 2 * k + 2, :], op=ALU.mult)
             ib = work.tile([P, 2, U], F32, name="ib", tag="ib")
-            nc.vector.tensor_tensor(out=ib[:], in0=a[:, :, 0:U], in1=a[:, :, 3 * U : G4], op=ALU.mult)
+            eng.tensor_tensor(out=ib[:], in0=a[:, :, 0:U], in1=a[:, :, 3 * U : G4], op=ALU.mult)
             c_sb = work.tile([P, 2, U], F32, name="c_sb", tag="c_sb")
-            nc.vector.tensor_tensor(out=c_sb[:], in0=fa[:], in1=ib[:], op=ALU.add)
+            eng.tensor_tensor(out=c_sb[:], in0=fa[:], in1=ib[:], op=ALU.add)
             nc.sync.dma_start(out=outv[1, :, 2 * k : 2 * k + 2, :], in_=c_sb[:])
+            c_of[k] = c_sb
+
+        def cell_tanh(k):
             tc_sb = work.tile([P, 2, U], F32, name="tc_sb", tag="tc_sb")
-            nc.scalar.activation(out=tc_sb[:], in_=c_sb[:], func=ACT.Tanh)
+            nc.scalar.activation(out=tc_sb[:], in_=c_of[k][:], func=ACT.Tanh)
             tc_of[k] = tc_sb
 
         def hidden(k):
@@ -217,13 +223,19 @@ def tile_lstm_kernel(tc, pre_layer, x, W_i, W_f, W_o, W_c, U_i, U_f, U_o, U_c, o
         flush_quant()
         for k in range(MX_AHEAD):
             mx_pair(k)
-        for s in range(NP + 2):
+        for s in range(NP + 3):
             if s < NP:
                 gates(2 * s)
                 gates(2 * s + 1)
             if 0 <= s - 1 < NP:
                 cell(s - 1)
-            if 0 <= s - 2 < NP:
+            if 0 <= s - 2 < G_PAIRS:
+                cell_tanh(s - 2)
+            if G_PAIRS <= s - 1 < NP:
+                cell_tanh(s - 1)
+            if 0 <= s - 3 < G_PAIRS:
+                hidden(s - 3)
+            if G_PAIRS <= s - 2 < NP:
                 hidden(s - 2)
             if state["front"] < NP:
                 front(FRONT_STEP)

@@ -15,23 +15,24 @@ ALU = mybir.AluOpType
 
 P = 128
 NT = 16
-NP = NT // 2
 D = 512
 U = 128
 G4 = 4 * U
 
+UNITS = [2, 2, 2, 2, 2, 2, 2, 1, 1]
+NU = len(UNITS)
+FIRST = [sum(UNITS[:u]) for u in range(NU)]
 MX_AHEAD = 2
 FRONT_FIRST = 3
 FRONT_STEP = 2
 H1_AT = 2
-G_PAIRS = 6
 
 
 def tile_lstm_kernel(tc, pre_layer, x, W_i, W_f, W_o, W_c, U_i, U_f, U_o, U_c, out):
     nc = tc.nc
     with ExitStack() as ctx:
         keep = ctx.enter_context(tc.tile_pool(name="keep", bufs=1))
-        work = ctx.enter_context(tc.tile_pool(name="work", bufs=5))
+        work = ctx.enter_context(tc.tile_pool(name="work", bufs=4))
         psum = ctx.enter_context(tc.psum_pool(name="psum", bufs=2))
         ctx.enter_context(tc.manual_schedule())
 
@@ -39,15 +40,16 @@ def tile_lstm_kernel(tc, pre_layer, x, W_i, W_f, W_o, W_c, U_i, U_f, U_o, U_c, o
         prev = pre_layer.rearrange("s (p t) u -> s p t u", t=NT)
         outv = out.rearrange("s (p t) u -> s p t u", t=NT)
 
-        x_sb = [keep.tile([P, 2 * D], BF16, name="x%d" % k) for k in range(NP)]
+        x_sb = [keep.tile([P, UNITS[u] * D], BF16, name="x%d" % u) for u in range(NU)]
         w_raw = [keep.tile([P, 4 * U], BF16, name="w_raw%d" % g) for g in range(4)]
         u_sb = keep.tile([P, G4], BF16, name="u_sb")
         ph_sb = [keep.tile([P, 8, U], BF16, name="ph%d" % i) for i in range(2)]
         pc_sb = keep.tile([P, NT, U], BF16, name="pc_sb")
 
-        def load_x(k):
+        def load_x(u):
+            n = UNITS[u]
             nc.sync.dma_start(
-                out=x_sb[k][:].rearrange("p (t k) -> p t k", t=2), in_=xv[:, 2 * k : 2 * k + 2, :]
+                out=x_sb[u][:].rearrange("p (t k) -> p t k", t=n), in_=xv[:, FIRST[u] : FIRST[u] + n, :]
             )
 
         load_x(0)
@@ -59,11 +61,11 @@ def tile_lstm_kernel(tc, pre_layer, x, W_i, W_f, W_o, W_c, U_i, U_f, U_o, U_c, o
             )
         for g, uw in enumerate((U_i, U_f, U_o, U_c)):
             nc.scalar.dma_start(out=u_sb[:, g * U : (g + 1) * U], in_=uw)
-        for k in (1, 2, 3, 4, 5):
-            load_x(k)
+        for u in (1, 2, 3, 4, 5):
+            load_x(u)
         nc.sync.dma_start(out=pc_sb[:], in_=prev[1])
-        load_x(6)
-        load_x(7)
+        for u in range(6, NU):
+            load_x(u)
         nc.sync.dma_start(out=ph_sb[1][:], in_=prev[0, :, 8:16, :])
 
         ident_f = keep.tile([P, P], F32, name="ident_f")
@@ -97,25 +99,29 @@ def tile_lstm_kernel(tc, pre_layer, x, W_i, W_f, W_o, W_c, U_i, U_f, U_o, U_c, o
 
         xg_of = {}
 
-        def x_front(k):
-            xt = psum.tile([P, 2, 2, P], F32, name="xt", tag="tr", bufs=2)
-            xw = x_sb[k][:].bitcast(F32)
-            for j in range(2):
-                for u in range(2):
-                    c0 = j * (D // 2) + u * P
-                    nc.tensor.transpose(xt[:, j, u, :], xw[:, c0 : c0 + P], ident_f[:])
-            xg = work.tile([P, 2 * D], BF16, name="xg", tag="xg", align_bytes=64)
-            dst = xg[:].bitcast(F32).rearrange("p (j r u) -> p j r u", j=2, r=P, u=2)
-            src = xt[:].rearrange("p j u r -> p j r u")
-            if k % 2 == 1:
+        def x_front(u):
+            n = UNITS[u]
+            xt = psum.tile([P, n, 2, P], F32, name="xt", tag="tr", bufs=2)
+            xw = x_sb[u][:].bitcast(F32)
+            for j in range(n):
+                for v in range(2):
+                    c0 = j * (D // 2) + v * P
+                    nc.tensor.transpose(xt[:, j, v, :], xw[:, c0 : c0 + P], ident_f[:])
+            xg = work.tile([P, n * D], BF16, name="xg", tag="xg", align_bytes=64)
+            dst = xg[:].bitcast(F32).rearrange("p (j r v) -> p j r v", j=n, r=P, v=2)
+            src = xt[:].rearrange("p j v r -> p j r v")
+            if u % 2 == 1:
                 nc.vector.tensor_copy(out=dst, in_=src)
             else:
                 nc.scalar.copy(out=dst, in_=src)
-            xg_of[k] = xg
+            xg_of[u] = xg
 
-        def x_quant(k):
-            cols = slice(2 * k * P, (2 * k + 2) * P)
-            nc.vector.quantize_mx(out=xq[:, cols].bitcast(FP8X4), scales=xs[:, cols], in_=xg_of[k][:])
+        def unit_cols(u):
+            return slice(FIRST[u] * P, (FIRST[u] + UNITS[u]) * P)
+
+        def x_quant(u):
+            cols = unit_cols(u)
+            nc.vector.quantize_mx(out=xq[:, cols].bitcast(FP8X4), scales=xs[:, cols], in_=xg_of[u][:])
 
         def h_half(i):
             ht = psum.tile([P, 8, P], BF16, name="ht", tag="tr", bufs=2)
@@ -125,12 +131,14 @@ def tile_lstm_kernel(tc, pre_layer, x, W_i, W_f, W_o, W_c, U_i, U_f, U_o, U_c, o
 
         mt_of = {}
 
-        def mx_pair(k):
-            cols = slice(2 * k * P, (2 * k + 2) * P)
-            for b in range(2):
-                mt = psum.tile([P, 2, 2 * P], F32, name="mt", tag="mt", bufs=3)
-                for gg in range(2):
-                    g = 2 * b + gg
+        def mx_unit(u):
+            n = UNITS[u]
+            cols = unit_cols(u)
+            per_bank = 4 // n
+            for b in range(n):
+                mt = psum.tile([P, per_bank, n * P], F32, name="mt", tag="mt", bufs=3)
+                for gg in range(per_bank):
+                    g = per_bank * b + gg
                     nc.tensor.matmul_mx(
                         out=mt[:, gg, :],
                         lhsT=wq[:, g * U : (g + 1) * U].bitcast(FP8X4),
@@ -140,61 +148,69 @@ def tile_lstm_kernel(tc, pre_layer, x, W_i, W_f, W_o, W_c, U_i, U_f, U_o, U_c, o
                         start=True,
                         stop=True,
                     )
-                mt_sb = work.tile([P, 2, 2 * P], F32, name="mt_sb%d" % b, tag="mt_sb%d" % b)
-                if b == 0 or k % 2 == 1:
+                mt_sb = work.tile([P, per_bank, n * P], F32, name="mt_sb%d" % b, tag="mt_sb%d" % b)
+                if b == 0:
                     nc.vector.tensor_copy(out=mt_sb[:], in_=mt[:])
                 else:
                     nc.scalar.copy(out=mt_sb[:], in_=mt[:])
-                mt_of[(k, b)] = mt_sb
+                mt_of[(u, b)] = mt_sb
 
         a_of = {}
 
-        def gates(t):
-            k, j = t // 2, t % 2
-            if j == 0:
-                a_new = work.tile([P, 2, G4], F32, name="a", tag="a")
-                a_of[k] = a_new
-            a = a_of[k]
-            zt = psum.tile([P, G4], F32, name="zt", tag="zt", bufs=3)
-            nc.tensor.matmul(
-                out=zt[:], lhsT=hT_sb[t // 8][:, (t % 8) * P : (t % 8 + 1) * P], rhs=u_sb[:], start=True, stop=False
-            )
-            for g in range(4):
+        def gates(u):
+            n = UNITS[u]
+            per_bank = 4 // n
+            a = work.tile([P, n, G4], F32, name="a", tag="a")
+            a_of[u] = a
+            zts = []
+            for j in range(n):
+                t = FIRST[u] + j
+                zt = psum.tile([P, G4], F32, name="zt", tag="zt", bufs=3)
                 nc.tensor.matmul(
-                    out=zt[:, g * U : (g + 1) * U],
-                    lhsT=mt_of[(k, g // 2)][:, g % 2, j * P : (j + 1) * P],
-                    rhs=ident_f[:],
-                    is_transpose=True,
-                    start=False,
-                    stop=(g == 3),
+                    out=zt[:],
+                    lhsT=hT_sb[t // 8][:, (t % 8) * P : (t % 8 + 1) * P],
+                    rhs=u_sb[:],
+                    start=True,
+                    stop=False,
                 )
-            nc.scalar.activation(out=a[:, j, 0 : 3 * U], in_=zt[:, 0 : 3 * U], func=ACT.Sigmoid)
-            nc.scalar.activation(out=a[:, j, 3 * U : G4], in_=zt[:, 3 * U : G4], func=ACT.Tanh)
+                zts.append(zt)
+            for j in range(n):
+                zt = zts[j]
+                for g in range(4):
+                    nc.tensor.matmul(
+                        out=zt[:, g * U : (g + 1) * U],
+                        lhsT=mt_of[(u, g // per_bank)][:, g % per_bank, j * P : (j + 1) * P],
+                        rhs=ident_f[:],
+                        is_transpose=True,
+                        start=False,
+                        stop=(g == 3),
+                    )
+                nc.scalar.activation(out=a[:, j, 0 : 3 * U], in_=zt[:, 0 : 3 * U], func=ACT.Sigmoid)
+                nc.scalar.activation(out=a[:, j, 3 * U : G4], in_=zt[:, 3 * U : G4], func=ACT.Tanh)
 
         tc_of = {}
-        c_of = {}
 
-        def cell(k):
-            eng = nc.gpsimd if k < G_PAIRS else nc.vector
-            a = a_of[k]
-            fa = work.tile([P, 2, U], F32, name="fa", tag="fa")
-            eng.tensor_tensor(out=fa[:], in0=a[:, :, U : 2 * U], in1=pc_sb[:, 2 * k : 2 * k + 2, :], op=ALU.mult)
-            ib = work.tile([P, 2, U], F32, name="ib", tag="ib")
-            eng.tensor_tensor(out=ib[:], in0=a[:, :, 0:U], in1=a[:, :, 3 * U : G4], op=ALU.mult)
-            c_sb = work.tile([P, 2, U], F32, name="c_sb", tag="c_sb")
-            eng.tensor_tensor(out=c_sb[:], in0=fa[:], in1=ib[:], op=ALU.add)
-            nc.sync.dma_start(out=outv[1, :, 2 * k : 2 * k + 2, :], in_=c_sb[:])
-            c_of[k] = c_sb
+        def cell(u):
+            n = UNITS[u]
+            rows = slice(FIRST[u], FIRST[u] + n)
+            a = a_of[u]
+            fa = work.tile([P, n, U], F32, name="fa", tag="fa")
+            nc.vector.tensor_tensor(out=fa[:], in0=a[:, :, U : 2 * U], in1=pc_sb[:, rows, :], op=ALU.mult)
+            ib = work.tile([P, n, U], F32, name="ib", tag="ib")
+            nc.vector.tensor_tensor(out=ib[:], in0=a[:, :, 0:U], in1=a[:, :, 3 * U : G4], op=ALU.mult)
+            c_sb = work.tile([P, n, U], F32, name="c_sb", tag="c_sb")
+            nc.vector.tensor_tensor(out=c_sb[:], in0=fa[:], in1=ib[:], op=ALU.add)
+            nc.sync.dma_start(out=outv[1, :, rows, :], in_=c_sb[:])
+            tc_sb = work.tile([P, n, U], F32, name="tc_sb", tag="tc_sb")
+            nc.scalar.activation(out=tc_sb[:], in_=c_sb[:], func=ACT.Tanh)
+            tc_of[u] = tc_sb
 
-        def cell_tanh(k):
-            tc_sb = work.tile([P, 2, U], F32, name="tc_sb", tag="tc_sb")
-            nc.scalar.activation(out=tc_sb[:], in_=c_of[k][:], func=ACT.Tanh)
-            tc_of[k] = tc_sb
-
-        def hidden(k):
-            h_sb = work.tile([P, 2, U], F32, name="h_sb", tag="h_sb")
-            nc.vector.tensor_tensor(out=h_sb[:], in0=a_of[k][:, :, 2 * U : 3 * U], in1=tc_of[k][:], op=ALU.mult)
-            nc.sync.dma_start(out=outv[0, :, 2 * k : 2 * k + 2, :], in_=h_sb[:])
+        def hidden(u):
+            n = UNITS[u]
+            rows = slice(FIRST[u], FIRST[u] + n)
+            h_sb = work.tile([P, n, U], F32, name="h_sb", tag="h_sb")
+            nc.vector.tensor_tensor(out=h_sb[:], in0=a_of[u][:, :, 2 * U : 3 * U], in1=tc_of[u][:], op=ALU.mult)
+            nc.sync.dma_start(out=outv[0, :, rows, :], in_=h_sb[:])
 
         for g in range(4):
             w_regroup(g)
@@ -206,7 +222,7 @@ def tile_lstm_kernel(tc, pre_layer, x, W_i, W_f, W_o, W_c, U_i, U_f, U_o, U_c, o
 
         def front(n):
             for i in range(n):
-                if state["front"] < NP:
+                if state["front"] < NU:
                     x_front(state["front"])
                     state["front"] += 1
                     if state["front"] - 1 > state["quant"]:
@@ -221,27 +237,20 @@ def tile_lstm_kernel(tc, pre_layer, x, W_i, W_f, W_o, W_c, U_i, U_f, U_o, U_c, o
         front(FRONT_FIRST)
         h_half(0)
         flush_quant()
-        for k in range(MX_AHEAD):
-            mx_pair(k)
-        for s in range(NP + 3):
-            if s < NP:
-                gates(2 * s)
-                gates(2 * s + 1)
-            if 0 <= s - 1 < NP:
+        for u in range(MX_AHEAD):
+            mx_unit(u)
+        for s in range(NU + 2):
+            if s < NU:
+                gates(s)
+            if 0 <= s - 1 < NU:
                 cell(s - 1)
-            if 0 <= s - 2 < G_PAIRS:
-                cell_tanh(s - 2)
-            if G_PAIRS <= s - 1 < NP:
-                cell_tanh(s - 1)
-            if 0 <= s - 3 < G_PAIRS:
-                hidden(s - 3)
-            if G_PAIRS <= s - 2 < NP:
+            if 0 <= s - 2 < NU:
                 hidden(s - 2)
-            if state["front"] < NP:
+            if state["front"] < NU:
                 front(FRONT_STEP)
-                if state["front"] >= NP:
+                if state["front"] >= NU:
                     flush_quant()
             if s == H1_AT:
                 h_half(1)
-            if s + MX_AHEAD < NP:
-                mx_pair(s + MX_AHEAD)
+            if s + MX_AHEAD < NU:
+                mx_unit(s + MX_AHEAD)

@@ -15,24 +15,24 @@ ALU = mybir.AluOpType
 
 P = 128
 NT = 16
+NP = NT // 2
 D = 512
 U = 128
 G4 = 4 * U
 
-UNITS = [2, 2, 2, 2, 2, 2, 2, 1, 1]
-NU = len(UNITS)
-FIRST = [sum(UNITS[:u]) for u in range(NU)]
 MX_AHEAD = 2
 FRONT_FIRST = 3
 FRONT_STEP = 2
 H1_AT = 2
+G_PAIRS = 5
+S_COPIES = 5
 
 
 def tile_lstm_kernel(tc, pre_layer, x, W_i, W_f, W_o, W_c, U_i, U_f, U_o, U_c, out):
     nc = tc.nc
     with ExitStack() as ctx:
         keep = ctx.enter_context(tc.tile_pool(name="keep", bufs=1))
-        work = ctx.enter_context(tc.tile_pool(name="work", bufs=4))
+        work = ctx.enter_context(tc.tile_pool(name="work", bufs=5))
         psum = ctx.enter_context(tc.psum_pool(name="psum", bufs=2))
         ctx.enter_context(tc.manual_schedule())
 
@@ -40,16 +40,15 @@ def tile_lstm_kernel(tc, pre_layer, x, W_i, W_f, W_o, W_c, U_i, U_f, U_o, U_c, o
         prev = pre_layer.rearrange("s (p t) u -> s p t u", t=NT)
         outv = out.rearrange("s (p t) u -> s p t u", t=NT)
 
-        x_sb = [keep.tile([P, UNITS[u] * D], BF16, name="x%d" % u) for u in range(NU)]
+        x_sb = [keep.tile([P, 2 * D], BF16, name="x%d" % k) for k in range(NP)]
         w_raw = [keep.tile([P, 4 * U], BF16, name="w_raw%d" % g) for g in range(4)]
         u_sb = keep.tile([P, G4], BF16, name="u_sb")
         ph_sb = [keep.tile([P, 8, U], BF16, name="ph%d" % i) for i in range(2)]
         pc_sb = keep.tile([P, NT, U], BF16, name="pc_sb")
 
-        def load_x(u):
-            n = UNITS[u]
+        def load_x(k):
             nc.sync.dma_start(
-                out=x_sb[u][:].rearrange("p (t k) -> p t k", t=n), in_=xv[:, FIRST[u] : FIRST[u] + n, :]
+                out=x_sb[k][:].rearrange("p (t k) -> p t k", t=2), in_=xv[:, 2 * k : 2 * k + 2, :]
             )
 
         load_x(0)
@@ -61,11 +60,11 @@ def tile_lstm_kernel(tc, pre_layer, x, W_i, W_f, W_o, W_c, U_i, U_f, U_o, U_c, o
             )
         for g, uw in enumerate((U_i, U_f, U_o, U_c)):
             nc.scalar.dma_start(out=u_sb[:, g * U : (g + 1) * U], in_=uw)
-        for u in (1, 2, 3, 4, 5):
-            load_x(u)
+        for k in (1, 2, 3, 4, 5):
+            load_x(k)
         nc.sync.dma_start(out=pc_sb[:], in_=prev[1])
-        for u in range(6, NU):
-            load_x(u)
+        load_x(6)
+        load_x(7)
         nc.sync.dma_start(out=ph_sb[1][:], in_=prev[0, :, 8:16, :])
 
         ident_f = keep.tile([P, P], F32, name="ident_f")
@@ -99,46 +98,40 @@ def tile_lstm_kernel(tc, pre_layer, x, W_i, W_f, W_o, W_c, U_i, U_f, U_o, U_c, o
 
         xg_of = {}
 
-        def x_front(u):
-            n = UNITS[u]
-            xt = psum.tile([P, n, 2, P], F32, name="xt", tag="tr", bufs=2)
-            xw = x_sb[u][:].bitcast(F32)
-            for j in range(n):
-                for v in range(2):
-                    c0 = j * (D // 2) + v * P
-                    nc.tensor.transpose(xt[:, j, v, :], xw[:, c0 : c0 + P], ident_f[:])
-            xg = work.tile([P, n * D], BF16, name="xg", tag="xg", align_bytes=64)
-            dst = xg[:].bitcast(F32).rearrange("p (j r v) -> p j r v", j=n, r=P, v=2)
-            src = xt[:].rearrange("p j v r -> p j r v")
-            if u % 2 == 1:
+        def x_front(k):
+            xt = psum.tile([P, 2, 2, P], F32, name="xt", tag="tz", bufs=4)
+            xw = x_sb[k][:].bitcast(F32)
+            for j in range(2):
+                for u in range(2):
+                    c0 = j * (D // 2) + u * P
+                    nc.tensor.transpose(xt[:, j, u, :], xw[:, c0 : c0 + P], ident_f[:])
+            xg = work.tile([P, 2 * D], BF16, name="xg", tag="xg", align_bytes=64)
+            dst = xg[:].bitcast(F32).rearrange("p (j r u) -> p j r u", j=2, r=P, u=2)
+            src = xt[:].rearrange("p j u r -> p j r u")
+            if k % 2 == 1:
                 nc.vector.tensor_copy(out=dst, in_=src)
             else:
                 nc.scalar.copy(out=dst, in_=src)
-            xg_of[u] = xg
+            xg_of[k] = xg
 
-        def unit_cols(u):
-            return slice(FIRST[u] * P, (FIRST[u] + UNITS[u]) * P)
-
-        def x_quant(u):
-            cols = unit_cols(u)
-            nc.vector.quantize_mx(out=xq[:, cols].bitcast(FP8X4), scales=xs[:, cols], in_=xg_of[u][:])
+        def x_quant(k):
+            cols = slice(2 * k * P, (2 * k + 2) * P)
+            nc.vector.quantize_mx(out=xq[:, cols].bitcast(FP8X4), scales=xs[:, cols], in_=xg_of[k][:])
 
         def h_half(i):
-            ht = psum.tile([P, 8, P], BF16, name="ht", tag="tr", bufs=2)
+            ht = psum.tile([P, 8, P], BF16, name="ht", tag="tz", bufs=4)
             for j in range(8):
                 nc.tensor.transpose(ht[:, j, :], ph_sb[i][:, j, :], ident_b[:])
             nc.scalar.copy(out=hT_sb[i][:], in_=ht[:].rearrange("p j r -> p (j r)"))
 
         mt_of = {}
 
-        def mx_unit(u):
-            n = UNITS[u]
-            cols = unit_cols(u)
-            per_bank = 4 // n
-            for b in range(n):
-                mt = psum.tile([P, per_bank, n * P], F32, name="mt", tag="mt", bufs=3)
-                for gg in range(per_bank):
-                    g = per_bank * b + gg
+        def mx_pair(k):
+            cols = slice(2 * k * P, (2 * k + 2) * P)
+            for b in range(2):
+                mt = psum.tile([P, 2, 2 * P], F32, name="mt", tag="mt", bufs=4)
+                for gg in range(2):
+                    g = 2 * b + gg
                     nc.tensor.matmul_mx(
                         out=mt[:, gg, :],
                         lhsT=wq[:, g * U : (g + 1) * U].bitcast(FP8X4),
@@ -148,69 +141,61 @@ def tile_lstm_kernel(tc, pre_layer, x, W_i, W_f, W_o, W_c, U_i, U_f, U_o, U_c, o
                         start=True,
                         stop=True,
                     )
-                mt_sb = work.tile([P, per_bank, n * P], F32, name="mt_sb%d" % b, tag="mt_sb%d" % b)
-                if b == 0:
+                mt_sb = work.tile([P, 2, 2 * P], F32, name="mt_sb%d" % b, tag="mt_sb%d" % b)
+                if b == 0 or k >= S_COPIES:
                     nc.vector.tensor_copy(out=mt_sb[:], in_=mt[:])
                 else:
                     nc.scalar.copy(out=mt_sb[:], in_=mt[:])
-                mt_of[(u, b)] = mt_sb
+                mt_of[(k, b)] = mt_sb
 
         a_of = {}
 
-        def gates(u):
-            n = UNITS[u]
-            per_bank = 4 // n
-            a = work.tile([P, n, G4], F32, name="a", tag="a")
-            a_of[u] = a
-            zts = []
-            for j in range(n):
-                t = FIRST[u] + j
-                zt = psum.tile([P, G4], F32, name="zt", tag="zt", bufs=3)
+        def gates(t):
+            k, j = t // 2, t % 2
+            if j == 0:
+                a_new = work.tile([P, 2, G4], F32, name="a", tag="a")
+                a_of[k] = a_new
+            a = a_of[k]
+            zt = psum.tile([P, G4], F32, name="zt", tag="tz", bufs=4)
+            nc.tensor.matmul(
+                out=zt[:], lhsT=hT_sb[t // 8][:, (t % 8) * P : (t % 8 + 1) * P], rhs=u_sb[:], start=True, stop=False
+            )
+            for g in range(4):
                 nc.tensor.matmul(
-                    out=zt[:],
-                    lhsT=hT_sb[t // 8][:, (t % 8) * P : (t % 8 + 1) * P],
-                    rhs=u_sb[:],
-                    start=True,
-                    stop=False,
+                    out=zt[:, g * U : (g + 1) * U],
+                    lhsT=mt_of[(k, g // 2)][:, g % 2, j * P : (j + 1) * P],
+                    rhs=ident_f[:],
+                    is_transpose=True,
+                    start=False,
+                    stop=(g == 3),
                 )
-                zts.append(zt)
-            for j in range(n):
-                zt = zts[j]
-                for g in range(4):
-                    nc.tensor.matmul(
-                        out=zt[:, g * U : (g + 1) * U],
-                        lhsT=mt_of[(u, g // per_bank)][:, g % per_bank, j * P : (j + 1) * P],
-                        rhs=ident_f[:],
-                        is_transpose=True,
-                        start=False,
-                        stop=(g == 3),
-                    )
-                nc.scalar.activation(out=a[:, j, 0 : 3 * U], in_=zt[:, 0 : 3 * U], func=ACT.Sigmoid)
-                nc.scalar.activation(out=a[:, j, 3 * U : G4], in_=zt[:, 3 * U : G4], func=ACT.Tanh)
+            nc.scalar.activation(out=a[:, j, 0 : 3 * U], in_=zt[:, 0 : 3 * U], func=ACT.Sigmoid)
+            nc.scalar.activation(out=a[:, j, 3 * U : G4], in_=zt[:, 3 * U : G4], func=ACT.Tanh)
 
         tc_of = {}
+        c_of = {}
 
-        def cell(u):
-            n = UNITS[u]
-            rows = slice(FIRST[u], FIRST[u] + n)
-            a = a_of[u]
-            fa = work.tile([P, n, U], F32, name="fa", tag="fa")
-            nc.vector.tensor_tensor(out=fa[:], in0=a[:, :, U : 2 * U], in1=pc_sb[:, rows, :], op=ALU.mult)
-            ib = work.tile([P, n, U], F32, name="ib", tag="ib")
-            nc.vector.tensor_tensor(out=ib[:], in0=a[:, :, 0:U], in1=a[:, :, 3 * U : G4], op=ALU.mult)
-            c_sb = work.tile([P, n, U], F32, name="c_sb", tag="c_sb")
-            nc.vector.tensor_tensor(out=c_sb[:], in0=fa[:], in1=ib[:], op=ALU.add)
-            nc.sync.dma_start(out=outv[1, :, rows, :], in_=c_sb[:])
-            tc_sb = work.tile([P, n, U], F32, name="tc_sb", tag="tc_sb")
-            nc.scalar.activation(out=tc_sb[:], in_=c_sb[:], func=ACT.Tanh)
-            tc_of[u] = tc_sb
+        def cell(k):
+            eng = nc.gpsimd if k < G_PAIRS else nc.vector
+            a = a_of[k]
+            fa = work.tile([P, 2, U], F32, name="fa", tag="fa")
+            eng.tensor_tensor(out=fa[:], in0=a[:, :, U : 2 * U], in1=pc_sb[:, 2 * k : 2 * k + 2, :], op=ALU.mult)
+            ib = work.tile([P, 2, U], F32, name="ib", tag="ib")
+            eng.tensor_tensor(out=ib[:], in0=a[:, :, 0:U], in1=a[:, :, 3 * U : G4], op=ALU.mult)
+            c_sb = work.tile([P, 2, U], F32, name="c_sb", tag="c_sb")
+            eng.tensor_tensor(out=c_sb[:], in0=fa[:], in1=ib[:], op=ALU.add)
+            nc.sync.dma_start(out=outv[1, :, 2 * k : 2 * k + 2, :], in_=c_sb[:])
+            c_of[k] = c_sb
 
-        def hidden(u):
-            n = UNITS[u]
-            rows = slice(FIRST[u], FIRST[u] + n)
-            h_sb = work.tile([P, n, U], F32, name="h_sb", tag="h_sb")
-            nc.vector.tensor_tensor(out=h_sb[:], in0=a_of[u][:, :, 2 * U : 3 * U], in1=tc_of[u][:], op=ALU.mult)
-            nc.sync.dma_start(out=outv[0, :, rows, :], in_=h_sb[:])
+        def cell_tanh(k):
+            tc_sb = work.tile([P, 2, U], F32, name="tc_sb", tag="tc_sb")
+            nc.scalar.activation(out=tc_sb[:], in_=c_of[k][:], func=ACT.Tanh)
+            tc_of[k] = tc_sb
+
+        def hidden(k):
+            h_sb = work.tile([P, 2, U], F32, name="h_sb", tag="h_sb")
+            nc.vector.tensor_tensor(out=h_sb[:], in0=a_of[k][:, :, 2 * U : 3 * U], in1=tc_of[k][:], op=ALU.mult)
+            nc.sync.dma_start(out=outv[0, :, 2 * k : 2 * k + 2, :], in_=h_sb[:])
 
         for g in range(4):
             w_regroup(g)
@@ -222,7 +207,7 @@ def tile_lstm_kernel(tc, pre_layer, x, W_i, W_f, W_o, W_c, U_i, U_f, U_o, U_c, o
 
         def front(n):
             for i in range(n):
-                if state["front"] < NU:
+                if state["front"] < NP:
                     x_front(state["front"])
                     state["front"] += 1
                     if state["front"] - 1 > state["quant"]:
@@ -237,20 +222,27 @@ def tile_lstm_kernel(tc, pre_layer, x, W_i, W_f, W_o, W_c, U_i, U_f, U_o, U_c, o
         front(FRONT_FIRST)
         h_half(0)
         flush_quant()
-        for u in range(MX_AHEAD):
-            mx_unit(u)
-        for s in range(NU + 2):
-            if s < NU:
-                gates(s)
-            if 0 <= s - 1 < NU:
+        for k in range(MX_AHEAD):
+            mx_pair(k)
+        for s in range(NP + 3):
+            if s < NP:
+                gates(2 * s)
+                gates(2 * s + 1)
+            if 0 <= s - 1 < NP:
                 cell(s - 1)
-            if 0 <= s - 2 < NU:
+            if 0 <= s - 2 < G_PAIRS:
+                cell_tanh(s - 2)
+            if G_PAIRS <= s - 1 < NP:
+                cell_tanh(s - 1)
+            if 0 <= s - 3 < G_PAIRS:
+                hidden(s - 3)
+            if G_PAIRS <= s - 2 < NP:
                 hidden(s - 2)
-            if state["front"] < NU:
+            if state["front"] < NP:
                 front(FRONT_STEP)
-                if state["front"] >= NU:
+                if state["front"] >= NP:
                     flush_quant()
             if s == H1_AT:
                 h_half(1)
-            if s + MX_AHEAD < NU:
-                mx_unit(s + MX_AHEAD)
+            if s + MX_AHEAD < NP:
+                mx_pair(s + MX_AHEAD)

@@ -24,8 +24,9 @@ MX_AHEAD = 2
 FRONT_FIRST = 3
 FRONT_STEP = 2
 H1_AT = 2
-G_PAIRS = 5
-S_COPIES = 5
+G_PAIRS = 6
+S_COPIES = 0
+V_ADD = (1, 3, 5)
 
 
 def tile_lstm_kernel(tc, pre_layer, x, W_i, W_f, W_o, W_c, U_i, U_f, U_o, U_c, out):
@@ -126,7 +127,43 @@ def tile_lstm_kernel(tc, pre_layer, x, W_i, W_f, W_o, W_c, U_i, U_f, U_o, U_c, o
 
         mt_of = {}
 
+        z_of = {}
+
+        def mx_pair_plain_sum(k):
+            mxs = []
+            for j in range(2):
+                t = 2 * k + j
+                cols = slice(t * P, (t + 1) * P)
+                mx = psum.tile([P, G4], F32, name="mx", tag="mt", bufs=4)
+                nc.tensor.matmul_mx(
+                    out=mx[:],
+                    lhsT=xq[:, cols].bitcast(FP8X4),
+                    lhsT_scale=xs[:, cols],
+                    rhs=wq[:].bitcast(FP8X4),
+                    rhs_scale=ws[:],
+                    start=True,
+                    stop=True,
+                )
+                mxs.append(mx)
+            pps = []
+            for j in range(2):
+                t = 2 * k + j
+                pp = psum.tile([P, G4], F32, name="pp", tag="tz", bufs=4)
+                nc.tensor.matmul(
+                    out=pp[:], lhsT=hT_sb[t // 8][:, (t % 8) * P : (t % 8 + 1) * P], rhs=u_sb[:], start=True, stop=True
+                )
+                pps.append(pp)
+            z_sb = work.tile([P, 2, G4], F32, name="z_sb", tag="z_sb")
+            for j in range(2):
+                nc.scalar.copy(out=z_sb[:, j, :], in_=pps[j][:])
+            for j in range(2):
+                nc.vector.tensor_tensor(out=z_sb[:, j, :], in0=mxs[j][:], in1=z_sb[:, j, :], op=ALU.add)
+            z_of[k] = z_sb
+
         def mx_pair(k):
+            if k in V_ADD:
+                mx_pair_plain_sum(k)
+                return
             cols = slice(2 * k * P, (2 * k + 2) * P)
             for b in range(2):
                 mt = psum.tile([P, 2, 2 * P], F32, name="mt", tag="mt", bufs=4)
@@ -156,6 +193,12 @@ def tile_lstm_kernel(tc, pre_layer, x, W_i, W_f, W_o, W_c, U_i, U_f, U_o, U_c, o
                 a_new = work.tile([P, 2, G4], F32, name="a", tag="a")
                 a_of[k] = a_new
             a = a_of[k]
+            if k in V_ADD:
+                if j == 0:
+                    z_sb = z_of[k]
+                    nc.scalar.activation(out=a[:, :, 0 : 3 * U], in_=z_sb[:, :, 0 : 3 * U], func=ACT.Sigmoid)
+                    nc.scalar.activation(out=a[:, :, 3 * U : G4], in_=z_sb[:, :, 3 * U : G4], func=ACT.Tanh)
+                return
             zt = psum.tile([P, G4], F32, name="zt", tag="tz", bufs=4)
             nc.tensor.matmul(
                 out=zt[:], lhsT=hT_sb[t // 8][:, (t % 8) * P : (t % 8 + 1) * P], rhs=u_sb[:], start=True, stop=False

@@ -24,9 +24,9 @@ MX_AHEAD = 2
 FRONT_FIRST = 3
 FRONT_STEP = 2
 H1_AT = 2
-G_PAIRS = 6
-S_COPIES = 0
-V_ADD = (1, 3, 5)
+G_PAIRS = 5
+X_ON_SCALAR = 5
+S_COPIES = 5
 
 
 def tile_lstm_kernel(tc, pre_layer, x, W_i, W_f, W_o, W_c, U_i, U_f, U_o, U_c, out):
@@ -109,7 +109,7 @@ def tile_lstm_kernel(tc, pre_layer, x, W_i, W_f, W_o, W_c, U_i, U_f, U_o, U_c, o
             xg = work.tile([P, 2 * D], BF16, name="xg", tag="xg", align_bytes=64)
             dst = xg[:].bitcast(F32).rearrange("p (j r u) -> p j r u", j=2, r=P, u=2)
             src = xt[:].rearrange("p j u r -> p j r u")
-            if k % 2 == 1:
+            if k % 2 == 1 and k >= X_ON_SCALAR:
                 nc.vector.tensor_copy(out=dst, in_=src)
             else:
                 nc.scalar.copy(out=dst, in_=src)
@@ -127,43 +127,7 @@ def tile_lstm_kernel(tc, pre_layer, x, W_i, W_f, W_o, W_c, U_i, U_f, U_o, U_c, o
 
         mt_of = {}
 
-        z_of = {}
-
-        def mx_pair_plain_sum(k):
-            mxs = []
-            for j in range(2):
-                t = 2 * k + j
-                cols = slice(t * P, (t + 1) * P)
-                mx = psum.tile([P, G4], F32, name="mx", tag="mt", bufs=4)
-                nc.tensor.matmul_mx(
-                    out=mx[:],
-                    lhsT=xq[:, cols].bitcast(FP8X4),
-                    lhsT_scale=xs[:, cols],
-                    rhs=wq[:].bitcast(FP8X4),
-                    rhs_scale=ws[:],
-                    start=True,
-                    stop=True,
-                )
-                mxs.append(mx)
-            pps = []
-            for j in range(2):
-                t = 2 * k + j
-                pp = psum.tile([P, G4], F32, name="pp", tag="tz", bufs=4)
-                nc.tensor.matmul(
-                    out=pp[:], lhsT=hT_sb[t // 8][:, (t % 8) * P : (t % 8 + 1) * P], rhs=u_sb[:], start=True, stop=True
-                )
-                pps.append(pp)
-            z_sb = work.tile([P, 2, G4], F32, name="z_sb", tag="z_sb")
-            for j in range(2):
-                nc.scalar.copy(out=z_sb[:, j, :], in_=pps[j][:])
-            for j in range(2):
-                nc.vector.tensor_tensor(out=z_sb[:, j, :], in0=mxs[j][:], in1=z_sb[:, j, :], op=ALU.add)
-            z_of[k] = z_sb
-
         def mx_pair(k):
-            if k in V_ADD:
-                mx_pair_plain_sum(k)
-                return
             cols = slice(2 * k * P, (2 * k + 2) * P)
             for b in range(2):
                 mt = psum.tile([P, 2, 2 * P], F32, name="mt", tag="mt", bufs=4)
@@ -193,12 +157,6 @@ def tile_lstm_kernel(tc, pre_layer, x, W_i, W_f, W_o, W_c, U_i, U_f, U_o, U_c, o
                 a_new = work.tile([P, 2, G4], F32, name="a", tag="a")
                 a_of[k] = a_new
             a = a_of[k]
-            if k in V_ADD:
-                if j == 0:
-                    z_sb = z_of[k]
-                    nc.scalar.activation(out=a[:, :, 0 : 3 * U], in_=z_sb[:, :, 0 : 3 * U], func=ACT.Sigmoid)
-                    nc.scalar.activation(out=a[:, :, 3 * U : G4], in_=z_sb[:, :, 3 * U : G4], func=ACT.Tanh)
-                return
             zt = psum.tile([P, G4], F32, name="zt", tag="tz", bufs=4)
             nc.tensor.matmul(
                 out=zt[:], lhsT=hT_sb[t // 8][:, (t % 8) * P : (t % 8 + 1) * P], rhs=u_sb[:], start=True, stop=False

@@ -25,8 +25,8 @@ FRONT_FIRST = 3
 FRONT_STEP = 2
 H1_AT = 2
 G_PAIRS = 5
-X_ON_SCALAR = 5
 S_COPIES = 5
+V_ADD = (1,)
 
 
 def tile_lstm_kernel(tc, pre_layer, x, W_i, W_f, W_o, W_c, U_i, U_f, U_o, U_c, out):
@@ -109,7 +109,7 @@ def tile_lstm_kernel(tc, pre_layer, x, W_i, W_f, W_o, W_c, U_i, U_f, U_o, U_c, o
             xg = work.tile([P, 2 * D], BF16, name="xg", tag="xg", align_bytes=64)
             dst = xg[:].bitcast(F32).rearrange("p (j r u) -> p j r u", j=2, r=P, u=2)
             src = xt[:].rearrange("p j u r -> p j r u")
-            if k % 2 == 1 and k >= X_ON_SCALAR:
+            if k % 2 == 1:
                 nc.vector.tensor_copy(out=dst, in_=src)
             else:
                 nc.scalar.copy(out=dst, in_=src)
@@ -127,7 +127,43 @@ def tile_lstm_kernel(tc, pre_layer, x, W_i, W_f, W_o, W_c, U_i, U_f, U_o, U_c, o
 
         mt_of = {}
 
+        z_of = {}
+
+        def mx_pair_plain_sum(k):
+            mxs = []
+            for j in range(2):
+                t = 2 * k + j
+                cols = slice(t * P, (t + 1) * P)
+                mx = psum.tile([P, G4], F32, name="mx", tag="mt", bufs=4)
+                nc.tensor.matmul_mx(
+                    out=mx[:],
+                    lhsT=xq[:, cols].bitcast(FP8X4),
+                    lhsT_scale=xs[:, cols],
+                    rhs=wq[:].bitcast(FP8X4),
+                    rhs_scale=ws[:],
+                    start=True,
+                    stop=True,
+                )
+                mxs.append(mx)
+            pps = []
+            for j in range(2):
+                t = 2 * k + j
+                pp = psum.tile([P, G4], F32, name="pp", tag="tz", bufs=4)
+                nc.tensor.matmul(
+                    out=pp[:], lhsT=hT_sb[t // 8][:, (t % 8) * P : (t % 8 + 1) * P], rhs=u_sb[:], start=True, stop=True
+                )
+                pps.append(pp)
+            z_sb = work.tile([P, 2, G4], F32, name="z_sb", tag="z_sb")
+            for j in range(2):
+                nc.scalar.copy(out=z_sb[:, j, :], in_=pps[j][:])
+            for j in range(2):
+                nc.vector.tensor_tensor(out=z_sb[:, j, :], in0=mxs[j][:], in1=z_sb[:, j, :], op=ALU.add)
+            z_of[k] = z_sb
+
         def mx_pair(k):
+            if k in V_ADD:
+                mx_pair_plain_sum(k)
+                return
             cols = slice(2 * k * P, (2 * k + 2) * P)
             for b in range(2):
                 mt = psum.tile([P, 2, 2 * P], F32, name="mt", tag="mt", bufs=4)
@@ -157,6 +193,12 @@ def tile_lstm_kernel(tc, pre_layer, x, W_i, W_f, W_o, W_c, U_i, U_f, U_o, U_c, o
                 a_new = work.tile([P, 2, G4], F32, name="a", tag="a")
                 a_of[k] = a_new
             a = a_of[k]
+            if k in V_ADD:
+                if j == 0:
+                    z_sb = z_of[k]
+                    nc.scalar.activation(out=a[:, :, 0 : 3 * U], in_=z_sb[:, :, 0 : 3 * U], func=ACT.Sigmoid)
+                    nc.scalar.activation(out=a[:, :, 3 * U : G4], in_=z_sb[:, :, 3 * U : G4], func=ACT.Tanh)
+                return
             zt = psum.tile([P, G4], F32, name="zt", tag="tz", bufs=4)
             nc.tensor.matmul(
                 out=zt[:], lhsT=hT_sb[t // 8][:, (t % 8) * P : (t % 8 + 1) * P], rhs=u_sb[:], start=True, stop=False

from contextlib import ExitStack

import concourse.mybir as mybir
from concourse.masks import make_identity

FLOPS = 2 * 2048 * 512 * 512 + 2 * 2048 * 128 * 512

F32 = mybir.dt.float32
BF16 = mybir.dt.bfloat16
U32 = mybir.dt.uint32
U8 = mybir.dt.uint8
FP8X4 = mybir.dt.float8_e4m3fn_x4
ACT = mybir.ActivationFunctionType
ALU = mybir.AluOpType

P = 128
NT = 16
NP = NT // 2
D = 512
U = 128
G4 = 4 * U

MX_AHEAD = 2
FRONT_FIRST = 3
FRONT_STEP = 2
H1_AT = 2
G_PAIRS = 5
S_COPIES = 5
V_ADD = (1,)


def tile_lstm_kernel(tc, pre_layer, x, W_i, W_f, W_o, W_c, U_i, U_f, U_o, U_c, out):
    nc = tc.nc
    with ExitStack() as ctx:
        keep = ctx.enter_context(tc.tile_pool(name="keep", bufs=1))
        work = ctx.enter_context(tc.tile_pool(name="work", bufs=5))
        psum = ctx.enter_context(tc.psum_pool(name="psum", bufs=2))
        ctx.enter_context(tc.manual_schedule())

        xv = x.rearrange("(p t) k -> p t k", t=NT)
        prev = pre_layer.rearrange("s (p t) u -> s p t u", t=NT)
        outv = out.rearrange("s (p t) u -> s p t u", t=NT)

        x_sb = [keep.tile([P, 2 * D], BF16, name="x%d" % k) for k in range(NP)]
        w_raw = [keep.tile([P, 4 * U], BF16, name="w_raw%d" % g) for g in range(4)]
        u_sb = keep.tile([P, G4], BF16, name="u_sb")
        ph_sb = [keep.tile([P, 8, U], BF16, name="ph%d" % i) for i in range(2)]
        pc_sb = keep.tile([P, NT, U], BF16, name="pc_sb")

        def load_x(k):
            nc.sync.dma_start(
                out=x_sb[k][:].rearrange("p (t k) -> p t k", t=2), in_=xv[:, 2 * k : 2 * k + 2, :]
            )

        load_x(0)
        nc.scalar.dma_start(out=ph_sb[0][:], in_=prev[0, :, 0:8, :])
        for g, w in enumerate((W_i, W_f, W_o, W_c)):
            nc.sync.dma_start(
                out=w_raw[g][:].rearrange("q (u m) -> q u m", u=2),
                in_=w.rearrange("(u q e) c -> q u (e c)", u=2, q=P, e=2),
            )
        for g, uw in enumerate((U_i, U_f, U_o, U_c)):
            nc.scalar.dma_start(out=u_sb[:, g * U : (g + 1) * U], in_=uw)
        for k in (1, 2, 3, 4, 5):
            load_x(k)
        nc.sync.dma_start(out=pc_sb[:], in_=prev[1])
        load_x(6)
        load_x(7)
        nc.sync.dma_start(out=ph_sb[1][:], in_=prev[0, :, 8:16, :])

        ident_f = keep.tile([P, P], F32, name="ident_f")
        make_identity(nc, ident_f[:])
        ident_b = keep.tile([P, P], BF16, name="ident_b")
        make_identity(nc, ident_b[:])
        warm = keep.tile([P, 1], F32, name="warm")
        nc.vector.memset(warm[:], 0.0)
        warm2 = keep.tile([P, 1], F32, name="warm2")
        nc.scalar.activation(out=warm2[:], in_=warm[:], func=ACT.Sigmoid)

        wg = keep.tile([P, 4 * G4], BF16, name="wg", align_bytes=64)
        wq = keep.tile([P, G4], U32, name="wq", align_bytes=64)
        ws = keep.tile([P, G4], U8, name="ws", align_bytes=64)
        xq = keep.tile([P, NT * P], U32, name="xq", align_bytes=64)
        xs = keep.tile([P, NT * P], U8, name="xs", align_bytes=64)
        hT_sb = [keep.tile([P, 8 * P], BF16, name="hT%d" % i) for i in range(2)]

        def w_regroup(g):
            nc.vector.tensor_copy(
                out=wg[:, g * 4 * U : (g + 1) * 4 * U].rearrange("p (c t) -> p c t", t=4),
                in_=w_raw[g][:].rearrange("p (t c) -> p c t", t=4),
            )

        def w_quant(g):
            nc.vector.quantize_mx(
                out=wq[:, g * U : (g + 1) * U].bitcast(FP8X4),
                scales=ws[:, g * U : (g + 1) * U],
                in_=wg[:, g * 4 * U : (g + 1) * 4 * U],
            )

        xg_of = {}

        def x_front(k):
            xt = psum.tile([P, 2, 2, P], F32, name="xt", tag="tz", bufs=4)
            xw = x_sb[k][:].bitcast(F32)
            for j in range(2):
                for u in range(2):
                    c0 = j * (D // 2) + u * P
                    nc.tensor.transpose(xt[:, j, u, :], xw[:, c0 : c0 + P], ident_f[:])
            xg = work.tile([P, 2 * D], BF16, name="xg", tag="xg", align_bytes=64)
            dst = xg[:].bitcast(F32).rearrange("p (j r u) -> p j r u", j=2, r=P, u=2)
            src = xt[:].rearrange("p j u r -> p j r u")
            if k % 2 == 1:
                nc.vector.tensor_copy(out=dst, in_=src)
            else:
                nc.scalar.copy(out=dst, in_=src)
            xg_of[k] = xg

        def x_quant(k):
            cols = slice(2 * k * P, (2 * k + 2) * P)
            nc.vector.quantize_mx(out=xq[:, cols].bitcast(FP8X4), scales=xs[:, cols], in_=xg_of[k][:])

        def h_half(i):
            ht = psum.tile([P, 8, P], BF16, name="ht", tag="tz", bufs=4)
            for j in range(8):
                nc.tensor.transpose(ht[:, j, :], ph_sb[i][:, j, :], ident_b[:])
            nc.scalar.copy(out=hT_sb[i][:], in_=ht[:].rearrange("p j r -> p (j r)"))

        mt_of = {}

        z_of = {}

        def mx_pair_plain_sum(k):
            mxs = []
            for j in range(2):
                t = 2 * k + j
                cols = slice(t * P, (t + 1) * P)
                mx = psum.tile([P, G4], F32, name="mx", tag="mt", bufs=4)
                nc.tensor.matmul_mx(
                    out=mx[:],
                    lhsT=xq[:, cols].bitcast(FP8X4),
                    lhsT_scale=xs[:, cols],
                    rhs=wq[:].bitcast(FP8X4),
                    rhs_scale=ws[:],
                    start=True,
                    stop=True,
                )
                mxs.append(mx)
            pps = []
            for j in range(2):
                t = 2 * k + j
                pp = psum.tile([P, G4], F32, name="pp", tag="tz", bufs=4)
                nc.tensor.matmul(
                    out=pp[:], lhsT=hT_sb[t // 8][:, (t % 8) * P : (t % 8 + 1) * P], rhs=u_sb[:], start=True, stop=True
                )
                pps.append(pp)
            z_sb = work.tile([P, 2, G4], F32, name="z_sb", tag="z_sb")
            for j in range(2):
                nc.scalar.copy(out=z_sb[:, j, :], in_=pps[j][:])
            for j in range(2):
                nc.vector.tensor_tensor(out=z_sb[:, j, :], in0=mxs[j][:], in1=z_sb[:, j, :], op=ALU.add)
            z_of[k] = z_sb

        def mx_pair(k):
            if k in V_ADD:
                mx_pair_plain_sum(k)
                return
            cols = slice(2 * k * P, (2 * k + 2) * P)
            for b in range(2):
                mt = psum.tile([P, 2, 2 * P], F32, name="mt", tag="mt", bufs=4)
                for gg in range(2):
                    g = 2 * b + gg
                    nc.tensor.matmul_mx(
                        out=mt[:, gg, :],
                        lhsT=wq[:, g * U : (g + 1) * U].bitcast(FP8X4),
                        lhsT_scale=ws[:, g * U : (g + 1) * U],
                        rhs=xq[:, cols].bitcast(FP8X4),
                        rhs_scale=xs[:, cols],
                        start=True,
                        stop=True,
                    )
                mt_sb = work.tile([P, 2, 2 * P], F32, name="mt_sb%d" % b, tag="mt_sb%d" % b)
                if b == 0 or k >= S_COPIES:
                    nc.vector.tensor_copy(out=mt_sb[:], in_=mt[:])
                else:
                    nc.scalar.copy(out=mt_sb[:], in_=mt[:])
                mt_of[(k, b)] = mt_sb

        a_of = {}

        def gates(t):
            k, j = t // 2, t % 2
            if j == 0:
                a_new = work.tile([P, 2, G4], F32, name="a", tag="a")
                a_of[k] = a_new
            a = a_of[k]
            if k in V_ADD:
                if j == 0:
                    z_sb = z_of[k]
                    nc.scalar.activation(out=a[:, :, 0 : 3 * U], in_=z_sb[:, :, 0 : 3 * U], func=ACT.Sigmoid)
                    nc.scalar.activation(out=a[:, :, 3 * U : G4], in_=z_sb[:, :, 3 * U : G4], func=ACT.Tanh)
                return
            zt = psum.tile([P, G4], F32, name="zt", tag="tz", bufs=4)
            nc.tensor.matmul(
                out=zt[:], lhsT=hT_sb[t // 8][:, (t % 8) * P : (t % 8 + 1) * P], rhs=u_sb[:], start=True, stop=False
            )
            for g in range(4):
                nc.tensor.matmul(
                    out=zt[:, g * U : (g + 1) * U],
                    lhsT=mt_of[(k, g // 2)][:, g % 2, j * P : (j + 1) * P],
                    rhs=ident_f[:],
                    is_transpose=True,
                    start=False,
                    stop=(g == 3),
                )
            nc.scalar.activation(out=a[:, j, 0 : 3 * U], in_=zt[:, 0 : 3 * U], func=ACT.Sigmoid)
            nc.scalar.activation(out=a[:, j, 3 * U : G4], in_=zt[:, 3 * U : G4], func=ACT.Tanh)

        tc_of = {}
        c_of = {}

        def cell(k):
            eng = nc.gpsimd if k < G_PAIRS else nc.vector
            a = a_of[k]
            fa = work.tile([P, 2, U], F32, name="fa", tag="fa")
            eng.tensor_tensor(out=fa[:], in0=a[:, :, U : 2 * U], in1=pc_sb[:, 2 * k : 2 * k + 2, :], op=ALU.mult)
            ib = work.tile([P, 2, U], F32, name="ib", tag="ib")
            eng.tensor_tensor(out=ib[:], in0=a[:, :, 0:U], in1=a[:, :, 3 * U : G4], op=ALU.mult)
            c_sb = work.tile([P, 2, U], F32, name="c_sb", tag="c_sb")
            eng.tensor_tensor(out=c_sb[:], in0=fa[:], in1=ib[:], op=ALU.add)
            nc.sync.dma_start(out=outv[1, :, 2 * k : 2 * k + 2, :], in_=c_sb[:])
            c_of[k] = c_sb

        def cell_tanh(k):
            tc_sb = work.tile([P, 2, U], F32, name="tc_sb", tag="tc_sb")
            nc.scalar.activation(out=tc_sb[:], in_=c_of[k][:], func=ACT.Tanh)
            tc_of[k] = tc_sb

        def hidden(k):
            h_sb = work.tile([P, 2, U], F32, name="h_sb", tag="h_sb")
            nc.vector.tensor_tensor(out=h_sb[:], in0=a_of[k][:, :, 2 * U : 3 * U], in1=tc_of[k][:], op=ALU.mult)
            nc.sync.dma_start(out=outv[0, :, 2 * k : 2 * k + 2, :], in_=h_sb[:])

        for g in range(4):
            w_regroup(g)
            if g > 0:
                w_quant(g - 1)
        w_quant(3)

        state = {"front": 0, "quant": 0}

        def front(n):
            for i in range(n):
                if state["front"] < NP:
                    x_front(state["front"])
                    state["front"] += 1
                    if state["front"] - 1 > state["quant"]:
                        x_quant(state["quant"])
                        state["quant"] += 1

        def flush_quant():
            while state["quant"] < state["front"]:
                x_quant(state["quant"])
                state["quant"] += 1

        front(FRONT_FIRST)
        h_half(0)
        flush_quant()
        for k in range(MX_AHEAD):
            mx_pair(k)
        for s in range(NP + 3):
            if s < NP:
                gates(2 * s)
                gates(2 * s + 1)
            if 0 <= s - 1 < NP:
                cell(s - 1)
            if 0 <= s - 2 < G_PAIRS:
                cell_tanh(s - 2)
            if G_PAIRS <= s - 1 < NP:
                cell_tanh(s - 1)
            if 0 <= s - 3 < G_PAIRS:
                hidden(s - 3)
            if G_PAIRS <= s - 2 < NP:
                hidden(s - 2)
            if state["front"] < NP:
                front(FRONT_STEP)
                if state["front"] >= NP:
                    flush_quant()
            if s == H1_AT:
                h_half(1)
            if s + MX_AHEAD < NP:
                mx_pair(s + MX_AHEAD)
